import numpy as np
import ml_dtypes


def mxq(x, axis, fmt="e4m3"):
    dtype, down = {"e4m3": (ml_dtypes.float8_e4m3fn, 7), "e5m2": (ml_dtypes.float8_e5m2, 14)}[fmt]
    v = np.moveaxis(np.asarray(x, np.float32).astype(ml_dtypes.bfloat16).astype(np.float64), axis, -1)
    blocks = v.reshape(v.shape[:-1] + (-1, 32))
    amax = np.abs(blocks).max(-1, keepdims=True)
    byte = np.maximum(np.where(amax > 0, np.frexp(amax)[1] - 1 + 127, 0) - down, 1)
    scale = np.exp2(byte - 127.0)
    codes = (blocks / scale).astype(np.float32).astype(dtype).astype(np.float64)
    return np.moveaxis((codes * scale).reshape(v.shape), -1, axis)


WIDE = False


def mx_kscale(k):
    if not WIDE:
        return np.ones(k)
    levels = np.array([10, -10, 5, -5, 0])
    if k % 512:
        return np.exp2(np.random.permutation(np.resize(levels, k // 32))).repeat(32)
    a = np.empty((k // 512, 16))
    for p in range(k // 512):
        a[p, :8] = np.random.permutation(np.resize(levels, 8))
        for g in range(8):
            far = levels[np.abs(levels - a[p, g]) >= 10]
            a[p, g + 8] = far[np.random.randint(len(far))]
    return np.exp2(a.ravel()).repeat(32)


BF16 = ml_dtypes.bfloat16


def bf(x):
    return np.asarray(x, np.float32).astype(BF16)


def f64(x):
    return np.asarray(x).astype(np.float64)


B, Q, K, D = 8, 1024, 512, 256
C = D + D


def setup_inputs():
    s, t = mx_kscale(K), mx_kscale(C)
    z = np.exp(2.0 * np.random.standard_normal((B, Q, K)))
    return {"attn_weights": bf(z / z.sum(-1, keepdims=True) * s),
            "context": bf(np.random.standard_normal((B, K, D)) * 0.5 / s[:, None] * t[:D]),
            "q": bf(np.random.standard_normal((B, Q, D)) * 4.0 / np.sqrt(D) * t[D:]),
            "W_out": bf(np.random.standard_normal((D, C)) * 6.0 / np.sqrt(C) / t),
            "b_out": bf(np.random.standard_normal(D) * 0.2)}


def reference(attn_weights, context, q, W_out, b_out):
    mix = mxq(f64(attn_weights), 2, "e4m3") @ mxq(f64(context), 1, "e4m3")
    combined = np.concatenate([mix, f64(q)], axis=-1)
    return np.tanh((mxq(combined, 2, "e4m3") @ mxq(f64(W_out), 1, "e4m3").T) + f64(b_out))

@@ -1,0 +1,241 @@
+from contextlib import ExitStack
+
+import concourse.mybir as mybir
+from concourse.masks import make_identity
+
+BF16 = mybir.dt.bfloat16
+F32 = mybir.dt.float32
+U32 = mybir.dt.uint32
+U8 = mybir.dt.uint8
+FP8X4 = mybir.dt.float8_e4m3fn_x4
+TANH = mybir.ActivationFunctionType.Tanh
+ADD = mybir.AluOpType.add
+
+B, Q, K, D = 8, 1024, 512, 256
+C = D + D
+FLOPS = 2 * B * Q * K * D + 2 * B * Q * C * D
+
+P = 128
+PACK = 4
+BATCH_TILES = Q // P
+UNIT_TILES = 2
+UNIT_ROWS = UNIT_TILES * P
+UNITS_PER_BATCH = BATCH_TILES // UNIT_TILES
+UNITS = B * UNITS_PER_BATCH
+LOAD_UNITS = 2
+LOAD_TILES = LOAD_UNITS * UNIT_TILES
+LOADS_PER_BATCH = BATCH_TILES // LOAD_TILES
+
+LAG_QUANTISE_A = 1
+LAG_MIX = 2
+LAG_TURN_COMB = 3
+LAG_QUANTISE_COMB = 4
+LAG_OUT = 5
+LAG_TANH = 6
+W_STEP = 3
+
+
+def tile_attention_pb_t_kernel(tc, attn_weights, context, q, W_out, b_out, out):
+    nc = tc.nc
+    with ExitStack() as stack:
+        stack.enter_context(tc.manual_schedule())
+        const = stack.enter_context(tc.tile_pool(name="const", bufs=1))
+        loads = stack.enter_context(tc.tile_pool(name="loads", bufs=1))
+        work = stack.enter_context(tc.tile_pool(name="work", bufs=4))
+        psum = stack.enter_context(tc.psum_pool(name="psum", bufs=2))
+
+        a_raws, rows_raws, ctx_raws = [], [], []
+        w_raw = const.tile([P, D // P, C], BF16)
+        bias_bf16 = const.tile([P, D], BF16)
+        for batch in range(B):
+            a_rows = attn_weights[batch].rearrange("(p t) k -> p t k", t=BATCH_TILES)
+            q_rows = q[batch].rearrange("(p t) d -> p t d", t=BATCH_TILES)
+            for part in range(LOADS_PER_BATCH):
+                first = part * LOAD_TILES
+                a_raw = loads.tile([P, LOAD_TILES, K], BF16, tag="a_raw", bufs=B * LOADS_PER_BATCH)
+                rows_raw = loads.tile([P, LOAD_TILES, C], BF16, tag="rows_raw", bufs=B * LOADS_PER_BATCH)
+                cuts = LOAD_UNITS if (batch, part) == (0, 0) else 1
+                width = LOAD_TILES // cuts
+                for cut in range(cuts):
+                    nc.sync.dma_start(
+                        out=a_raw[:, cut * width : (cut + 1) * width, :],
+                        in_=a_rows[:, first + cut * width : first + (cut + 1) * width, :],
+                    )
+                    if cut == 0 and part == 0:
+                        ctx_raw = loads.tile([P, PACK, D], BF16, tag="ctx_raw", bufs=B)
+                        nc.sync.dma_start(out=ctx_raw[:], in_=context[batch].rearrange("(p t) d -> p t d", t=PACK))
+                        ctx_raws.append(ctx_raw)
+                nc.sync.dma_start(out=rows_raw[:, :, D:C], in_=q_rows[:, first : first + LOAD_TILES, :])
+                a_raws.append(a_raw)
+                rows_raws.append(rows_raw)
+                if (batch, part) == (0, 0):
+                    nc.sync.dma_start(out=w_raw[:], in_=W_out.rearrange("(j p) c -> p j c", p=P))
+                    nc.sync.dma_start(out=bias_bf16[:], in_=b_out.partition_broadcast(P))
+
+        warm = const.tile([P, 1], F32)
+        nc.vector.memset(warm[:], 0.0)
+        nc.scalar.activation(out=warm[:], in_=warm[:], func=TANH)
+
+        ident = const.tile([P, P], F32)
+        make_identity(nc, ident[:])
+
+        w_grouped = const.tile([P, D, PACK], BF16, align_bytes=64)
+        w_codes = const.tile([P, D], U32, align_bytes=64)
+        w_scales = const.tile([P, D], U8, align_bytes=64)
+        bias = const.tile([P, D], F32)
+
+        def prepare_w():
+            w_words = w_raw[:].bitcast(F32)
+            w_t = psum.tile([P, 2, D], F32, tag="a_t")
+            for j in range(D // P):
+                for u in range(2):
+                    nc.tensor.transpose(w_t[:, u, j * P : (j + 1) * P], w_words[:, j, u : C // 2 : 2], ident[:])
+            nc.vector.tensor_copy(out=w_grouped[:].bitcast(F32), in_=w_t[:].rearrange("p u o -> p o u"))
+            nc.vector.tensor_copy(out=bias[:], in_=bias_bf16[:])
+            nc.vector.quantize_mx(
+                out=w_codes[:].bitcast(FP8X4), scales=w_scales[:], in_=w_grouped[:].rearrange("p o t -> p (o t)")
+            )
+
+        a_t, a_grouped, a_codes, a_scales = {}, {}, {}, {}
+        ctx_grouped, ctx_codes, ctx_scales = {}, {}, {}
+        mix, comb_t, comb, comb_codes, comb_scales = {}, {}, {}, {}, {}
+        out_acc, result = {}, {}
+
+        def turn(raw, unit, tag):
+            words = raw[:].bitcast(F32)
+            turned = psum.tile([P, 2, UNIT_ROWS], F32, tag=tag)
+            for i in range(UNIT_TILES):
+                j = (unit % LOAD_UNITS) * UNIT_TILES + i
+                for u in range(2):
+                    nc.tensor.transpose(turned[:, u, i * P : (i + 1) * P], words[:, j, u : C // 2 : 2], ident[:])
+            return turned
+
+        def turn_a(unit):
+            turned = turn(a_raws[unit // LOAD_UNITS], unit, "a_t")
+            a_t[unit] = turned
+
+        def copy_a_out(unit):
+            grouped = work.tile([P, UNIT_ROWS, PACK], BF16, tag="a_grouped", align_bytes=64)
+            nc.scalar.copy(out=grouped[:].bitcast(F32), in_=a_t[unit][:].rearrange("p u r -> p r u"))
+            a_grouped[unit] = grouped
+
+        def quantise_a(unit):
+            codes = work.tile([P, UNIT_ROWS], U32, tag="a_codes", align_bytes=64)
+            scales = work.tile([P, UNIT_ROWS], U8, tag="a_scales", align_bytes=64)
+            nc.vector.quantize_mx(
+                out=codes[:].bitcast(FP8X4),
+                scales=scales[:],
+                in_=a_grouped[unit][:].rearrange("p r t -> p (r t)"),
+            )
+            a_codes[unit], a_scales[unit] = codes, scales
+
+        def regroup_context(batch):
+            grouped = work.tile([P, D, PACK], BF16, tag="ctx_grouped", bufs=2, align_bytes=64)
+            nc.vector.tensor_copy(out=grouped[:], in_=ctx_raws[batch][:].rearrange("p t d -> p d t"))
+            ctx_grouped[batch] = grouped
+
+        def quantise_context(batch):
+            codes = work.tile([P, D], U32, tag="ctx_codes", bufs=3, align_bytes=64)
+            scales = work.tile([P, D], U8, tag="ctx_scales", bufs=3, align_bytes=64)
+            nc.vector.quantize_mx(
+                out=codes[:].bitcast(FP8X4),
+                scales=scales[:],
+                in_=ctx_grouped[batch][:].rearrange("p d t -> p (d t)"),
+            )
+            ctx_codes[batch], ctx_scales[batch] = codes, scales
+
+        def multiply(codes, scales, right_codes, right_scales, tag):
+            acc = psum.tile([P, UNIT_TILES, D], F32, tag=tag)
+            for i in range(UNIT_TILES):
+                rows = slice(i * P, (i + 1) * P)
+                nc.tensor.matmul_mx(
+                    out=acc[:, i, :],
+                    lhsT=codes[:, rows].bitcast(FP8X4),
+                    lhsT_scale=scales[:, rows],
+                    rhs=right_codes[:].bitcast(FP8X4),
+                    rhs_scale=right_scales[:],
+                    start=True,
+                    stop=True,
+                )
+            return acc
+
+        def multiply_mix(unit):
+            batch = unit // UNITS_PER_BATCH
+            acc = multiply(a_codes[unit], a_scales[unit], ctx_codes[batch], ctx_scales[batch], "mix")
+            mix[unit] = acc
+
+        def copy_mix_out(unit):
+            load, part = divmod(unit, LOAD_UNITS)
+            tiles = slice(part * UNIT_TILES, (part + 1) * UNIT_TILES)
+            nc.scalar.copy(out=rows_raws[load][:, tiles, 0:D], in_=mix[unit][:])
+
+        def turn_comb(unit):
+            turned = turn(rows_raws[unit // LOAD_UNITS], unit, "comb_t")
+            comb_t[unit] = turned
+
+        def copy_comb_out(unit):
+            grouped = work.tile([P, UNIT_ROWS, PACK], BF16, tag="comb", align_bytes=64)
+            dst, src = grouped[:].bitcast(F32), comb_t[unit][:].rearrange("p u r -> p r u")
+            if unit % UNITS_PER_BATCH == UNITS_PER_BATCH - 1:
+                nc.scalar.copy(out=dst, in_=src)
+            else:
+                nc.vector.tensor_copy(out=dst, in_=src)
+            comb[unit] = grouped
+
+        def quantise_comb(unit):
+            codes = work.tile([P, UNIT_ROWS], U32, tag="comb_codes", align_bytes=64)
+            scales = work.tile([P, UNIT_ROWS], U8, tag="comb_scales", align_bytes=64)
+            nc.vector.quantize_mx(
+                out=codes[:].bitcast(FP8X4),
+                scales=scales[:],
+                in_=comb[unit][:].rearrange("p r t -> p (r t)"),
+            )
+            comb_codes[unit], comb_scales[unit] = codes, scales
+
+        def multiply_out(unit):
+            acc = multiply(comb_codes[unit], comb_scales[unit], w_codes, w_scales, "out_acc")
+            out_acc[unit] = acc
+
+        def add_bias(unit):
+            summed = work.tile([P, UNIT_TILES, D], F32, tag="result", bufs=8)
+            nc.vector.tensor_tensor(
+                out=summed[:],
+                in0=out_acc[unit][:],
+                in1=bias[:].unsqueeze(1).to_broadcast([P, UNIT_TILES, D]),
+                op=ADD,
+            )
+            result[unit] = summed
+
+        def tanh_and_store(unit):
+            batch, part = divmod(unit, UNITS_PER_BATCH)
+            tiles = slice(part * UNIT_TILES, (part + 1) * UNIT_TILES)
+            nc.scalar.activation(out=result[unit][:], in_=result[unit][:], func=TANH)
+            nc.sync.dma_start(
+                out=out[batch].rearrange("(p t) o -> p t o", t=BATCH_TILES)[:, tiles, :],
+                in_=result[unit][:],
+            )
+
+        def run(stage, unit):
+            if 0 <= unit < UNITS:
+                stage(unit)
+
+        def run_for_batch(stage, unit):
+            if unit % UNITS_PER_BATCH == 0:
+                run(lambda first_unit: stage(first_unit // UNITS_PER_BATCH), unit)
+
+        for step in range(UNITS + LAG_TANH):
+            if step == W_STEP:
+                prepare_w()
+            run(turn_a, step)
+            run(turn_comb, step - LAG_TURN_COMB)
+            run(multiply_mix, step - LAG_MIX)
+            run(multiply_out, step - LAG_OUT)
+            run(copy_a_out, step)
+            run(copy_comb_out, step - LAG_TURN_COMB)
+            run_for_batch(regroup_context, step)
+            run(quantise_a, step - LAG_QUANTISE_A)
+            run(tanh_and_store, step - LAG_TANH)
+            run(copy_mix_out, step - LAG_MIX)
+            run(add_bias, step - LAG_OUT)
+            run_for_batch(quantise_context, step - 1)
+            run(quantise_comb, step - LAG_QUANTISE_COMB)

@@ -33,6 +33,8 @@ LAG_QUANTISE_COMB = 4
 LAG_OUT = 5
 LAG_TANH = 6
 W_STEP = 3
+WARM_HEAD = 6
+WARM_STEPS = 6
 
 
 def tile_attention_pb_t_kernel(tc, attn_weights, context, q, W_out, b_out, out):
@@ -78,6 +80,16 @@ def tile_attention_pb_t_kernel(tc, attn_weights, context, q, W_out, b_out, out):
 
         ident = const.tile([P, P], F32)
         make_identity(nc, ident[:])
+
+        ones = const.tile([P, 512], BF16)
+        nc.vector.memset(ones[:], 1.0)
+
+        def dummy_matmuls(count):
+            scratch = psum.tile([P, 512], F32, tag="out_acc")
+            for i in range(count):
+                nc.tensor.matmul(scratch[:], lhsT=ones[:, 0:P], rhs=ones[:], start=True, stop=True)
+
+        dummy_matmuls(WARM_HEAD)
 
         w_grouped = const.tile([P, D, PACK], BF16, align_bytes=64)
         w_codes = const.tile([P, D], U32, align_bytes=64)
@@ -228,6 +240,8 @@ def tile_attention_pb_t_kernel(tc, attn_weights, context, q, W_out, b_out, out):
                 prepare_w()
             run(turn_a, step)
             run(turn_comb, step - LAG_TURN_COMB)
+            if step < WARM_STEPS:
+                dummy_matmuls(1)
             run(multiply_mix, step - LAG_MIX)
             run(multiply_out, step - LAG_OUT)
             run(copy_a_out, step)

@@ -26,15 +26,14 @@ LOAD_UNITS = 2
 LOAD_TILES = LOAD_UNITS * UNIT_TILES
 LOADS_PER_BATCH = BATCH_TILES // LOAD_TILES
 
-LAG_QUANTISE_A = 1
+STEP_UNITS = 2
 LAG_MIX = 2
 LAG_TURN_COMB = 3
-LAG_QUANTISE_COMB = 4
-LAG_OUT = 5
-LAG_TANH = 6
-W_STEP = 3
+LAG_OUT = 4
+LAG_TANH = 5
+W_STEP = 2
 WARM_HEAD = 6
-WARM_STEPS = 6
+WARM_STEPS = 4
 
 
 def tile_attention_pb_t_kernel(tc, attn_weights, context, q, W_out, b_out, out):
@@ -43,7 +42,7 @@ def tile_attention_pb_t_kernel(tc, attn_weights, context, q, W_out, b_out, out):
         stack.enter_context(tc.manual_schedule())
         const = stack.enter_context(tc.tile_pool(name="const", bufs=1))
         loads = stack.enter_context(tc.tile_pool(name="loads", bufs=1))
-        work = stack.enter_context(tc.tile_pool(name="work", bufs=4))
+        work = stack.enter_context(tc.tile_pool(name="work", bufs=6))
         psum = stack.enter_context(tc.psum_pool(name="psum", bufs=2))
 
         a_raws, rows_raws, ctx_raws = [], [], []
@@ -209,7 +208,7 @@ def tile_attention_pb_t_kernel(tc, attn_weights, context, q, W_out, b_out, out):
             out_acc[unit] = acc
 
         def add_bias(unit):
-            summed = work.tile([P, UNIT_TILES, D], F32, tag="result", bufs=8)
+            summed = work.tile([P, UNIT_TILES, D], F32, tag="result", bufs=14)
             nc.vector.tensor_tensor(
                 out=summed[:],
                 in0=out_acc[unit][:],
@@ -227,15 +226,15 @@ def tile_attention_pb_t_kernel(tc, attn_weights, context, q, W_out, b_out, out):
                 in_=result[unit][:],
             )
 
-        def run(stage, unit):
-            if 0 <= unit < UNITS:
-                stage(unit)
+        def run(stage, step):
+            for unit in range(STEP_UNITS * step, STEP_UNITS * (step + 1)):
+                if 0 <= unit < UNITS:
+                    stage(unit)
 
-        def run_for_batch(stage, unit):
-            if unit % UNITS_PER_BATCH == 0:
-                run(lambda first_unit: stage(first_unit // UNITS_PER_BATCH), unit)
+        def run_for_batch(stage, step):
+            run(lambda unit: stage(unit // UNITS_PER_BATCH) if unit % UNITS_PER_BATCH == 0 else None, step)
 
-        for step in range(UNITS + LAG_TANH):
+        for step in range(UNITS // STEP_UNITS + LAG_TANH):
             if step == W_STEP:
                 prepare_w()
             run(turn_a, step)
@@ -245,11 +244,11 @@ def tile_attention_pb_t_kernel(tc, attn_weights, context, q, W_out, b_out, out):
             run(multiply_mix, step - LAG_MIX)
             run(multiply_out, step - LAG_OUT)
             run(copy_a_out, step)
-            run(copy_comb_out, step - LAG_TURN_COMB)
-            run_for_batch(regroup_context, step)
-            run(quantise_a, step - LAG_QUANTISE_A)
             run(tanh_and_store, step - LAG_TANH)
             run(copy_mix_out, step - LAG_MIX)
+            run(copy_comb_out, step - LAG_TURN_COMB)
+            run_for_batch(regroup_context, step)
+            run(quantise_a, step)
             run(add_bias, step - LAG_OUT)
             run_for_batch(quantise_context, step - 1)
-            run(quantise_comb, step - LAG_QUANTISE_COMB)
+            run(quantise_comb, step - LAG_TURN_COMB)

@@ -27,8 +27,9 @@ LOAD_TILES = LOAD_UNITS * UNIT_TILES
 LOADS_PER_BATCH = BATCH_TILES // LOAD_TILES
 
 STEP_UNITS = 2
-LAG_MIX = 2
-LAG_TURN_COMB = 3
+LAG_MIX = 1
+LAG_TURN_COMB = 2
+LAG_QUANTISE_COMB = 3
 LAG_OUT = 4
 LAG_TANH = 5
 W_STEP = 2
@@ -238,17 +239,17 @@ def tile_attention_pb_t_kernel(tc, attn_weights, context, q, W_out, b_out, out):
             if step == W_STEP:
                 prepare_w()
             run(turn_a, step)
-            run(turn_comb, step - LAG_TURN_COMB)
             if step < WARM_STEPS:
                 dummy_matmuls(1)
             run(multiply_mix, step - LAG_MIX)
+            run(turn_comb, step - LAG_TURN_COMB)
             run(multiply_out, step - LAG_OUT)
             run(copy_a_out, step)
-            run(tanh_and_store, step - LAG_TANH)
             run(copy_mix_out, step - LAG_MIX)
-            run(copy_comb_out, step - LAG_TURN_COMB)
+            run(tanh_and_store, step - LAG_TANH)
+            run(quantise_comb, step - LAG_QUANTISE_COMB)
             run_for_batch(regroup_context, step)
             run(quantise_a, step)
+            run(copy_comb_out, step - LAG_TURN_COMB)
+            run_for_batch(quantise_context, step)
             run(add_bias, step - LAG_OUT)
-            run_for_batch(quantise_context, step - 1)
-            run(quantise_comb, step - LAG_TURN_COMB)

@@ -48,7 +48,8 @@ def tile_attention_pb_t_kernel(tc, attn_weights, context, q, W_out, b_out, out):
 
         a_raws, rows_raws, ctx_raws = [], [], []
         w_raw = const.tile([P, D // P, C], BF16)
-        bias_bf16 = const.tile([P, D], BF16)
+        bias_row = const.tile([P, D], BF16)
+        nc.vector.memset(bias_row[:], 0.0)
         for batch in range(B):
             a_rows = attn_weights[batch].rearrange("(p t) k -> p t k", t=BATCH_TILES)
             q_rows = q[batch].rearrange("(p t) d -> p t d", t=BATCH_TILES)
@@ -72,7 +73,7 @@ def tile_attention_pb_t_kernel(tc, attn_weights, context, q, W_out, b_out, out):
                 rows_raws.append(rows_raw)
                 if (batch, part) == (0, 0):
                     nc.sync.dma_start(out=w_raw[:], in_=W_out.rearrange("(j p) c -> p j c", p=P))
-                    nc.sync.dma_start(out=bias_bf16[:], in_=b_out.partition_broadcast(P))
+                    nc.sync.dma_start(out=bias_row[0:1, :], in_=b_out.unsqueeze(0))
 
         warm = const.tile([P, 1], F32)
         nc.vector.memset(warm[:], 0.0)
@@ -103,7 +104,9 @@ def tile_attention_pb_t_kernel(tc, attn_weights, context, q, W_out, b_out, out):
                 for u in range(2):
                     nc.tensor.transpose(w_t[:, u, j * P : (j + 1) * P], w_words[:, j, u : C // 2 : 2], ident[:])
             nc.vector.tensor_copy(out=w_grouped[:].bitcast(F32), in_=w_t[:].rearrange("p u o -> p o u"))
-            nc.vector.tensor_copy(out=bias[:], in_=bias_bf16[:])
+            bias_t = psum.tile([P, D], F32, tag="a_t")
+            nc.tensor.matmul(bias_t[:], lhsT=ones[:, 0:P], rhs=bias_row[:], start=True, stop=True)
+            nc.vector.tensor_copy(out=bias[:], in_=bias_t[:])
             nc.vector.quantize_mx(
                 out=w_codes[:].bitcast(FP8X4), scales=w_scales[:], in_=w_grouped[:].rearrange("p o t -> p (o t)")
             )

@@ -26,14 +26,15 @@ LOAD_UNITS = 2
 LOAD_TILES = LOAD_UNITS * UNIT_TILES
 LOADS_PER_BATCH = BATCH_TILES // LOAD_TILES
 
-STEP_UNITS = 2
+GROUPS = [[0], [1]] + [[unit, unit + 1] for unit in range(2, UNITS - 2, 2)] + [[UNITS - 2], [UNITS - 1]]
 LAG_MIX = 1
 LAG_TURN_COMB = 2
 LAG_QUANTISE_COMB = 3
 LAG_OUT = 4
-LAG_TANH = 5
+LAG_BIAS = 5
+LAG_TANH = 6
 W_STEP = 2
-WARM_HEAD = 6
+WARM_HEAD = 3
 WARM_STEPS = 4
 
 
@@ -43,7 +44,7 @@ def tile_attention_pb_t_kernel(tc, attn_weights, context, q, W_out, b_out, out):
         stack.enter_context(tc.manual_schedule())
         const = stack.enter_context(tc.tile_pool(name="const", bufs=1))
         loads = stack.enter_context(tc.tile_pool(name="loads", bufs=1))
-        work = stack.enter_context(tc.tile_pool(name="work", bufs=6))
+        work = stack.enter_context(tc.tile_pool(name="work", bufs=3))
         psum = stack.enter_context(tc.psum_pool(name="psum", bufs=2))
 
         a_raws, rows_raws, ctx_raws = [], [], []
@@ -129,20 +130,33 @@ def tile_attention_pb_t_kernel(tc, attn_weights, context, q, W_out, b_out, out):
             turned = turn(a_raws[unit // LOAD_UNITS], unit, "a_t")
             a_t[unit] = turned
 
-        def copy_a_out(unit):
-            grouped = work.tile([P, UNIT_ROWS, PACK], BF16, tag="a_grouped", align_bytes=64)
-            nc.scalar.copy(out=grouped[:].bitcast(F32), in_=a_t[unit][:].rearrange("p u r -> p r u"))
-            a_grouped[unit] = grouped
+        def rows_of(group, unit):
+            first = (unit - group[0]) * UNIT_ROWS
+            return slice(first, first + UNIT_ROWS)
 
-        def quantise_a(unit):
-            codes = work.tile([P, UNIT_ROWS], U32, tag="a_codes", align_bytes=64)
-            scales = work.tile([P, UNIT_ROWS], U8, tag="a_scales", align_bytes=64)
+        def quantise(grouped, group, tag):
+            rows = len(group) * UNIT_ROWS
+            codes = work.tile([P, rows], U32, tag=tag + "_codes", align_bytes=64)
+            scales = work.tile([P, rows], U8, tag=tag + "_scales", align_bytes=64)
             nc.vector.quantize_mx(
-                out=codes[:].bitcast(FP8X4),
-                scales=scales[:],
-                in_=a_grouped[unit][:].rearrange("p r t -> p (r t)"),
+                out=codes[:].bitcast(FP8X4), scales=scales[:], in_=grouped[:].rearrange("p r t -> p (r t)")
             )
-            a_codes[unit], a_scales[unit] = codes, scales
+            return codes, scales
+
+        def turn_group_a(group):
+            for unit in group:
+                turn_a(unit)
+
+        def copy_a_out(group):
+            grouped = work.tile([P, len(group) * UNIT_ROWS, PACK], BF16, tag="a_grouped", bufs=2, align_bytes=64)
+            for unit in group:
+                dst = grouped[:, rows_of(group, unit), :].bitcast(F32)
+                nc.scalar.copy(out=dst, in_=a_t[unit][:].rearrange("p u r -> p r u"))
+            a_grouped[group[0]] = grouped
+
+        def quantise_a(group):
+            codes, scales = quantise(a_grouped[group[0]], group, "a")
+            a_codes[group[0]], a_scales[group[0]] = codes, scales
 
         def regroup_context(batch):
             grouped = work.tile([P, D, PACK], BF16, tag="ctx_grouped", bufs=2, align_bytes=64)
@@ -159,10 +173,10 @@ def tile_attention_pb_t_kernel(tc, attn_weights, context, q, W_out, b_out, out):
             )
             ctx_codes[batch], ctx_scales[batch] = codes, scales
 
-        def multiply(codes, scales, right_codes, right_scales, tag):
+        def multiply(codes, scales, first_row, right_codes, right_scales, tag):
             acc = psum.tile([P, UNIT_TILES, D], F32, tag=tag)
             for i in range(UNIT_TILES):
-                rows = slice(i * P, (i + 1) * P)
+                rows = slice(first_row + i * P, first_row + (i + 1) * P)
                 nc.tensor.matmul_mx(
                     out=acc[:, i, :],
                     lhsT=codes[:, rows].bitcast(FP8X4),
@@ -174,74 +188,83 @@ def tile_attention_pb_t_kernel(tc, attn_weights, context, q, W_out, b_out, out):
                 )
             return acc
 
-        def multiply_mix(unit):
-            batch = unit // UNITS_PER_BATCH
-            acc = multiply(a_codes[unit], a_scales[unit], ctx_codes[batch], ctx_scales[batch], "mix")
-            mix[unit] = acc
+        def multiply_mix(group):
+            for unit in group:
+                batch = unit // UNITS_PER_BATCH
+                first_row = rows_of(group, unit).start
+                acc = multiply(
+                    a_codes[group[0]], a_scales[group[0]], first_row, ctx_codes[batch], ctx_scales[batch], "mix"
+                )
+                mix[unit] = acc
 
-        def copy_mix_out(unit):
-            load, part = divmod(unit, LOAD_UNITS)
-            tiles = slice(part * UNIT_TILES, (part + 1) * UNIT_TILES)
-            nc.scalar.copy(out=rows_raws[load][:, tiles, 0:D], in_=mix[unit][:])
+        def copy_mix_out(group):
+            for unit in group:
+                load, part = divmod(unit, LOAD_UNITS)
+                tiles = slice(part * UNIT_TILES, (part + 1) * UNIT_TILES)
+                nc.scalar.copy(out=rows_raws[load][:, tiles, 0:D], in_=mix[unit][:])
 
-        def turn_comb(unit):
-            turned = turn(rows_raws[unit // LOAD_UNITS], unit, "comb_t")
-            comb_t[unit] = turned
+        def turn_comb(group):
+            for unit in group:
+                turned = turn(rows_raws[unit // LOAD_UNITS], unit, "comb_t")
+                comb_t[unit] = turned
 
-        def copy_comb_out(unit):
-            grouped = work.tile([P, UNIT_ROWS, PACK], BF16, tag="comb", align_bytes=64)
-            dst, src = grouped[:].bitcast(F32), comb_t[unit][:].rearrange("p u r -> p r u")
-            if unit % UNITS_PER_BATCH == UNITS_PER_BATCH - 1:
-                nc.scalar.copy(out=dst, in_=src)
-            else:
-                nc.vector.tensor_copy(out=dst, in_=src)
-            comb[unit] = grouped
+        def copy_comb_out(group):
+            grouped = work.tile([P, len(group) * UNIT_ROWS, PACK], BF16, tag="comb", bufs=3, align_bytes=64)
+            for unit in group:
+                dst = grouped[:, rows_of(group, unit), :].bitcast(F32)
+                src = comb_t[unit][:].rearrange("p u r -> p r u")
+                if unit % UNITS_PER_BATCH == UNITS_PER_BATCH - 1:
+                    nc.scalar.copy(out=dst, in_=src)
+                else:
+                    nc.vector.tensor_copy(out=dst, in_=src)
+            comb[group[0]] = grouped
 
-        def quantise_comb(unit):
-            codes = work.tile([P, UNIT_ROWS], U32, tag="comb_codes", align_bytes=64)
-            scales = work.tile([P, UNIT_ROWS], U8, tag="comb_scales", align_bytes=64)
-            nc.vector.quantize_mx(
-                out=codes[:].bitcast(FP8X4),
-                scales=scales[:],
-                in_=comb[unit][:].rearrange("p r t -> p (r t)"),
-            )
-            comb_codes[unit], comb_scales[unit] = codes, scales
+        def quantise_comb(group):
+            codes, scales = quantise(comb[group[0]], group, "comb")
+            comb_codes[group[0]], comb_scales[group[0]] = codes, scales
 
-        def multiply_out(unit):
-            acc = multiply(comb_codes[unit], comb_scales[unit], w_codes, w_scales, "out_acc")
-            out_acc[unit] = acc
+        def multiply_out(group):
+            for unit in group:
+                first_row = rows_of(group, unit).start
+                acc = multiply(comb_codes[group[0]], comb_scales[group[0]], first_row, w_codes, w_scales, "out_acc")
+                out_acc[unit] = acc
 
-        def add_bias(unit):
-            summed = work.tile([P, UNIT_TILES, D], F32, tag="result", bufs=14)
-            nc.vector.tensor_tensor(
-                out=summed[:],
-                in0=out_acc[unit][:],
-                in1=bias[:].unsqueeze(1).to_broadcast([P, UNIT_TILES, D]),
-                op=ADD,
-            )
-            result[unit] = summed
+        def add_bias(group):
+            summed = work.tile([P, len(group) * UNIT_TILES, D], F32, tag="result", bufs=7)
+            for unit in group:
+                first = (unit - group[0]) * UNIT_TILES
+                nc.vector.tensor_tensor(
+                    out=summed[:, first : first + UNIT_TILES, :],
+                    in0=out_acc[unit][:],
+                    in1=bias[:].unsqueeze(1).to_broadcast([P, UNIT_TILES, D]),
+                    op=ADD,
+                )
+            result[group[0]] = summed
 
-        def tanh_and_store(unit):
-            batch, part = divmod(unit, UNITS_PER_BATCH)
-            tiles = slice(part * UNIT_TILES, (part + 1) * UNIT_TILES)
-            nc.scalar.activation(out=result[unit][:], in_=result[unit][:], func=TANH)
+        def tanh_and_store(group):
+            batch, part = divmod(group[0], UNITS_PER_BATCH)
+            tiles = slice(part * UNIT_TILES, (part + len(group)) * UNIT_TILES)
+            summed = result[group[0]]
+            nc.scalar.activation(out=summed[:], in_=summed[:], func=TANH)
             nc.sync.dma_start(
                 out=out[batch].rearrange("(p t) o -> p t o", t=BATCH_TILES)[:, tiles, :],
-                in_=result[unit][:],
+                in_=summed[:],
             )
 
         def run(stage, step):
-            for unit in range(STEP_UNITS * step, STEP_UNITS * (step + 1)):
-                if 0 <= unit < UNITS:
-                    stage(unit)
+            if 0 <= step < len(GROUPS):
+                stage(GROUPS[step])
 
         def run_for_batch(stage, step):
-            run(lambda unit: stage(unit // UNITS_PER_BATCH) if unit % UNITS_PER_BATCH == 0 else None, step)
+            if 0 <= step < len(GROUPS):
+                for unit in GROUPS[step]:
+                    if unit % UNITS_PER_BATCH == 0:
+                        stage(unit // UNITS_PER_BATCH)
 
-        for step in range(UNITS // STEP_UNITS + LAG_TANH):
+        for step in range(len(GROUPS) + LAG_TANH):
             if step == W_STEP:
                 prepare_w()
-            run(turn_a, step)
+            run(turn_group_a, step)
             if step < WARM_STEPS:
                 dummy_matmuls(1)
             run(multiply_mix, step - LAG_MIX)
@@ -249,10 +272,10 @@ def tile_attention_pb_t_kernel(tc, attn_weights, context, q, W_out, b_out, out):
             run(multiply_out, step - LAG_OUT)
             run(copy_a_out, step)
             run(copy_mix_out, step - LAG_MIX)
+            run(add_bias, step - LAG_BIAS)
             run(tanh_and_store, step - LAG_TANH)
-            run(quantise_comb, step - LAG_QUANTISE_COMB)
             run_for_batch(regroup_context, step)
+            run(quantise_comb, step - LAG_QUANTISE_COMB)
+            run_for_batch(quantise_context, step)
             run(quantise_a, step)
             run(copy_comb_out, step - LAG_TURN_COMB)
-            run_for_batch(quantise_context, step)
-            run(add_bias, step - LAG_OUT)

@@ -10,6 +10,7 @@ U8 = mybir.dt.uint8
 FP8X4 = mybir.dt.float8_e4m3fn_x4
 TANH = mybir.ActivationFunctionType.Tanh
 ADD = mybir.AluOpType.add
+MULT = mybir.AluOpType.mult
 
 B, Q, K, D = 8, 1024, 512, 256
 C = D + D
@@ -34,6 +35,7 @@ LAG_OUT = 4
 LAG_BIAS = 5
 LAG_TANH = 6
 W_STEP = 2
+CTX_PIECES = 4
 WARM_HEAD = 3
 WARM_STEPS = 4
 
@@ -100,12 +102,12 @@ def tile_attention_pb_t_kernel(tc, attn_weights, context, q, W_out, b_out, out):
 
         def prepare_w():
             w_words = w_raw[:].bitcast(F32)
-            w_t = psum.tile([P, 2, D], F32, tag="a_t")
+            w_t = psum.tile([P, 2, D], F32, tag="out_acc")
             for j in range(D // P):
                 for u in range(2):
                     nc.tensor.transpose(w_t[:, u, j * P : (j + 1) * P], w_words[:, j, u : C // 2 : 2], ident[:])
             nc.vector.tensor_copy(out=w_grouped[:].bitcast(F32), in_=w_t[:].rearrange("p u o -> p o u"))
-            bias_t = psum.tile([P, D], F32, tag="a_t")
+            bias_t = psum.tile([P, D], F32, tag="out_acc")
             nc.tensor.matmul(bias_t[:], lhsT=ones[:, 0:P], rhs=bias_row[:], start=True, stop=True)
             nc.vector.tensor_copy(out=bias[:], in_=bias_t[:])
             nc.vector.quantize_mx(
@@ -160,7 +162,15 @@ def tile_attention_pb_t_kernel(tc, attn_weights, context, q, W_out, b_out, out):
 
         def regroup_context(batch):
             grouped = work.tile([P, D, PACK], BF16, tag="ctx_grouped", bufs=2, align_bytes=64)
-            nc.vector.tensor_copy(out=grouped[:], in_=ctx_raws[batch][:].rearrange("p t d -> p d t"))
+            src = ctx_raws[batch][:].rearrange("p t d -> p d t")
+            if batch == 0:
+                nc.vector.tensor_copy(out=grouped[:], in_=src)
+            else:
+                for piece in range(CTX_PIECES):
+                    feats = slice(piece * D // CTX_PIECES, (piece + 1) * D // CTX_PIECES)
+                    nc.gpsimd.tensor_scalar(
+                        out=grouped[:, feats, :], in0=src[:, feats, :], scalar1=1.0, scalar2=0.0, op0=MULT, op1=ADD
+                    )
             ctx_grouped[batch] = grouped
 
         def quantise_context(batch):
@@ -213,7 +223,7 @@ def tile_attention_pb_t_kernel(tc, attn_weights, context, q, W_out, b_out, out):
             for unit in group:
                 dst = grouped[:, rows_of(group, unit), :].bitcast(F32)
                 src = comb_t[unit][:].rearrange("p u r -> p r u")
-                if unit % UNITS_PER_BATCH == UNITS_PER_BATCH - 1:
+                if unit % 5 == 0:
                     nc.scalar.copy(out=dst, in_=src)
                 else:
                     nc.vector.tensor_copy(out=dst, in_=src)
@@ -231,25 +241,29 @@ def tile_attention_pb_t_kernel(tc, attn_weights, context, q, W_out, b_out, out):
 
         def add_bias(group):
             summed = work.tile([P, len(group) * UNIT_TILES, D], F32, tag="result", bufs=7)
+            width = 1 if group == GROUPS[-1] else UNIT_TILES
             for unit in group:
-                first = (unit - group[0]) * UNIT_TILES
-                nc.vector.tensor_tensor(
-                    out=summed[:, first : first + UNIT_TILES, :],
-                    in0=out_acc[unit][:],
-                    in1=bias[:].unsqueeze(1).to_broadcast([P, UNIT_TILES, D]),
-                    op=ADD,
-                )
+                for i in range(0, UNIT_TILES, width):
+                    first = (unit - group[0]) * UNIT_TILES + i
+                    nc.vector.tensor_tensor(
+                        out=summed[:, first : first + width, :],
+                        in0=out_acc[unit][:, i : i + width, :],
+                        in1=bias[:].unsqueeze(1).to_broadcast([P, width, D]),
+                        op=ADD,
+                    )
             result[group[0]] = summed
 
         def tanh_and_store(group):
             batch, part = divmod(group[0], UNITS_PER_BATCH)
-            tiles = slice(part * UNIT_TILES, (part + len(group)) * UNIT_TILES)
+            out_rows = out[batch].rearrange("(p t) o -> p t o", t=BATCH_TILES)
             summed = result[group[0]]
-            nc.scalar.activation(out=summed[:], in_=summed[:], func=TANH)
-            nc.sync.dma_start(
-                out=out[batch].rearrange("(p t) o -> p t o", t=BATCH_TILES)[:, tiles, :],
-                in_=summed[:],
-            )
+            tiles = len(group) * UNIT_TILES
+            width = 1 if group == GROUPS[-1] else tiles
+            for i in range(0, tiles, width):
+                piece = summed[:, i : i + width, :]
+                nc.scalar.activation(out=piece, in_=piece, func=TANH)
+                first = part * UNIT_TILES + i
+                nc.sync.dma_start(out=out_rows[:, first : first + width, :], in_=piece)
 
         def run(stage, step):
             if 0 <= step < len(GROUPS):
@@ -274,7 +288,7 @@ def tile_attention_pb_t_kernel(tc, attn_weights, context, q, W_out, b_out, out):
             run(copy_mix_out, step - LAG_MIX)
             run(add_bias, step - LAG_BIAS)
             run(tanh_and_store, step - LAG_TANH)
-            run_for_batch(regroup_context, step)
+            run_for_batch(regroup_context, step if step == 0 else step + 2)
             run(quantise_comb, step - LAG_QUANTISE_COMB)
             run_for_batch(quantise_context, step)
             run(quantise_a, step)

@@ -185,6 +185,8 @@ def tile_attention_pb_t_kernel(tc, attn_weights, context, q, W_out, b_out, out):
 
         def multiply(codes, scales, first_row, right_codes, right_scales, tag):
             acc = psum.tile([P, UNIT_TILES, D], F32, tag=tag)
+            if first_row == 0:
+                nc.tensor.matmul(acc[:, 0, 0:P], lhsT=ones[:, 0:P], rhs=ones[:, 0:P], start=True, stop=True)
             for i in range(UNIT_TILES):
                 rows = slice(first_row + i * P, first_row + (i + 1) * P)
                 nc.tensor.matmul_mx(

from contextlib import ExitStack

import concourse.mybir as mybir
from concourse.masks import make_identity

BF16 = mybir.dt.bfloat16
F32 = mybir.dt.float32
U32 = mybir.dt.uint32
U8 = mybir.dt.uint8
FP8X4 = mybir.dt.float8_e4m3fn_x4
TANH = mybir.ActivationFunctionType.Tanh
ADD = mybir.AluOpType.add
MULT = mybir.AluOpType.mult

B, Q, K, D = 8, 1024, 512, 256
C = D + D
FLOPS = 2 * B * Q * K * D + 2 * B * Q * C * D

P = 128
PACK = 4
BATCH_TILES = Q // P
UNIT_TILES = 2
UNIT_ROWS = UNIT_TILES * P
UNITS_PER_BATCH = BATCH_TILES // UNIT_TILES
UNITS = B * UNITS_PER_BATCH
LOAD_UNITS = 2
LOAD_TILES = LOAD_UNITS * UNIT_TILES
LOADS_PER_BATCH = BATCH_TILES // LOAD_TILES

GROUPS = [[0], [1]] + [[unit, unit + 1] for unit in range(2, UNITS - 2, 2)] + [[UNITS - 2], [UNITS - 1]]
LAG_MIX = 1
LAG_TURN_COMB = 2
LAG_QUANTISE_COMB = 3
LAG_OUT = 4
LAG_BIAS = 5
LAG_TANH = 6
W_STEP = 2
CTX_PIECES = 4
WARM_HEAD = 3
WARM_STEPS = 4


def tile_attention_pb_t_kernel(tc, attn_weights, context, q, W_out, b_out, out):
    nc = tc.nc
    with ExitStack() as stack:
        stack.enter_context(tc.manual_schedule())
        const = stack.enter_context(tc.tile_pool(name="const", bufs=1))
        loads = stack.enter_context(tc.tile_pool(name="loads", bufs=1))
        work = stack.enter_context(tc.tile_pool(name="work", bufs=3))
        psum = stack.enter_context(tc.psum_pool(name="psum", bufs=2))

        a_raws, rows_raws, ctx_raws = [], [], []
        w_raw = const.tile([P, D // P, C], BF16)
        bias_row = const.tile([P, D], BF16)
        nc.vector.memset(bias_row[:], 0.0)
        for batch in range(B):
            a_rows = attn_weights[batch].rearrange("(p t) k -> p t k", t=BATCH_TILES)
            q_rows = q[batch].rearrange("(p t) d -> p t d", t=BATCH_TILES)
            for part in range(LOADS_PER_BATCH):
                first = part * LOAD_TILES
                a_raw = loads.tile([P, LOAD_TILES, K], BF16, tag="a_raw", bufs=B * LOADS_PER_BATCH)
                rows_raw = loads.tile([P, LOAD_TILES, C], BF16, tag="rows_raw", bufs=B * LOADS_PER_BATCH)
                cuts = LOAD_UNITS if (batch, part) == (0, 0) else 1
                width = LOAD_TILES // cuts
                for cut in range(cuts):
                    nc.sync.dma_start(
                        out=a_raw[:, cut * width : (cut + 1) * width, :],
                        in_=a_rows[:, first + cut * width : first + (cut + 1) * width, :],
                    )
                    if cut == 0 and part == 0:
                        ctx_raw = loads.tile([P, PACK, D], BF16, tag="ctx_raw", bufs=B)
                        nc.sync.dma_start(out=ctx_raw[:], in_=context[batch].rearrange("(p t) d -> p t d", t=PACK))
                        ctx_raws.append(ctx_raw)
                nc.sync.dma_start(out=rows_raw[:, :, D:C], in_=q_rows[:, first : first + LOAD_TILES, :])
                a_raws.append(a_raw)
                rows_raws.append(rows_raw)
                if (batch, part) == (0, 0):
                    nc.sync.dma_start(out=w_raw[:], in_=W_out.rearrange("(j p) c -> p j c", p=P))
                    nc.sync.dma_start(out=bias_row[0:1, :], in_=b_out.unsqueeze(0))

        warm = const.tile([P, 1], F32)
        nc.vector.memset(warm[:], 0.0)
        nc.scalar.activation(out=warm[:], in_=warm[:], func=TANH)

        ident = const.tile([P, P], F32)
        make_identity(nc, ident[:])

        ones = const.tile([P, 512], BF16)
        nc.vector.memset(ones[:], 1.0)

        def dummy_matmuls(count):
            scratch = psum.tile([P, 512], F32, tag="out_acc")
            for i in range(count):
                nc.tensor.matmul(scratch[:], lhsT=ones[:, 0:P], rhs=ones[:], start=True, stop=True)

        dummy_matmuls(WARM_HEAD)

        w_grouped = const.tile([P, D, PACK], BF16, align_bytes=64)
        w_codes = const.tile([P, D], U32, align_bytes=64)
        w_scales = const.tile([P, D], U8, align_bytes=64)
        bias = const.tile([P, D], F32)

        def prepare_w():
            w_words = w_raw[:].bitcast(F32)
            w_t = psum.tile([P, 2, D], F32, tag="out_acc")
            for j in range(D // P):
                for u in range(2):
                    nc.tensor.transpose(w_t[:, u, j * P : (j + 1) * P], w_words[:, j, u : C // 2 : 2], ident[:])
            nc.vector.tensor_copy(out=w_grouped[:].bitcast(F32), in_=w_t[:].rearrange("p u o -> p o u"))
            bias_t = psum.tile([P, D], F32, tag="out_acc")
            nc.tensor.matmul(bias_t[:], lhsT=ones[:, 0:P], rhs=bias_row[:], start=True, stop=True)
            nc.vector.tensor_copy(out=bias[:], in_=bias_t[:])
            nc.vector.quantize_mx(
                out=w_codes[:].bitcast(FP8X4), scales=w_scales[:], in_=w_grouped[:].rearrange("p o t -> p (o t)")
            )

        a_t, a_grouped, a_codes, a_scales = {}, {}, {}, {}
        ctx_grouped, ctx_codes, ctx_scales = {}, {}, {}
        mix, comb_t, comb, comb_codes, comb_scales = {}, {}, {}, {}, {}
        out_acc, result = {}, {}

        def turn(raw, unit, tag):
            words = raw[:].bitcast(F32)
            turned = psum.tile([P, 2, UNIT_ROWS], F32, tag=tag)
            for i in range(UNIT_TILES):
                j = (unit % LOAD_UNITS) * UNIT_TILES + i
                for u in range(2):
                    nc.tensor.transpose(turned[:, u, i * P : (i + 1) * P], words[:, j, u : C // 2 : 2], ident[:])
            return turned

        def turn_a(unit):
            turned = turn(a_raws[unit // LOAD_UNITS], unit, "a_t")
            a_t[unit] = turned

        def rows_of(group, unit):
            first = (unit - group[0]) * UNIT_ROWS
            return slice(first, first + UNIT_ROWS)

        def quantise(grouped, group, tag):
            rows = len(group) * UNIT_ROWS
            codes = work.tile([P, rows], U32, tag=tag + "_codes", align_bytes=64)
            scales = work.tile([P, rows], U8, tag=tag + "_scales", align_bytes=64)
            nc.vector.quantize_mx(
                out=codes[:].bitcast(FP8X4), scales=scales[:], in_=grouped[:].rearrange("p r t -> p (r t)")
            )
            return codes, scales

        def turn_group_a(group):
            for unit in group:
                turn_a(unit)

        def copy_a_out(group):
            grouped = work.tile([P, len(group) * UNIT_ROWS, PACK], BF16, tag="a_grouped", bufs=2, align_bytes=64)
            for unit in group:
                dst = grouped[:, rows_of(group, unit), :].bitcast(F32)
                nc.scalar.copy(out=dst, in_=a_t[unit][:].rearrange("p u r -> p r u"))
            a_grouped[group[0]] = grouped

        def quantise_a(group):
            codes, scales = quantise(a_grouped[group[0]], group, "a")
            a_codes[group[0]], a_scales[group[0]] = codes, scales

        def regroup_context(batch):
            grouped = work.tile([P, D, PACK], BF16, tag="ctx_grouped", bufs=2, align_bytes=64)
            src = ctx_raws[batch][:].rearrange("p t d -> p d t")
            if batch == 0:
                nc.vector.tensor_copy(out=grouped[:], in_=src)
            else:
                for piece in range(CTX_PIECES):
                    feats = slice(piece * D // CTX_PIECES, (piece + 1) * D // CTX_PIECES)
                    nc.gpsimd.tensor_scalar(
                        out=grouped[:, feats, :], in0=src[:, feats, :], scalar1=1.0, scalar2=0.0, op0=MULT, op1=ADD
                    )
            ctx_grouped[batch] = grouped

        def quantise_context(batch):
            codes = work.tile([P, D], U32, tag="ctx_codes", bufs=3, align_bytes=64)
            scales = work.tile([P, D], U8, tag="ctx_scales", bufs=3, align_bytes=64)
            nc.vector.quantize_mx(
                out=codes[:].bitcast(FP8X4),
                scales=scales[:],
                in_=ctx_grouped[batch][:].rearrange("p d t -> p (d t)"),
            )
            ctx_codes[batch], ctx_scales[batch] = codes, scales

        def multiply(codes, scales, first_row, right_codes, right_scales, tag):
            acc = psum.tile([P, UNIT_TILES, D], F32, tag=tag)
            if first_row == 0:
                nc.tensor.matmul(acc[:, 0, 0:P], lhsT=ones[:, 0:P], rhs=ones[:, 0:P], start=True, stop=True)
            for i in range(UNIT_TILES):
                rows = slice(first_row + i * P, first_row + (i + 1) * P)
                nc.tensor.matmul_mx(
                    out=acc[:, i, :],
                    lhsT=codes[:, rows].bitcast(FP8X4),
                    lhsT_scale=scales[:, rows],
                    rhs=right_codes[:].bitcast(FP8X4),
                    rhs_scale=right_scales[:],
                    start=True,
                    stop=True,
                )
            return acc

        def multiply_mix(group):
            for unit in group:
                batch = unit // UNITS_PER_BATCH
                first_row = rows_of(group, unit).start
                acc = multiply(
                    a_codes[group[0]], a_scales[group[0]], first_row, ctx_codes[batch], ctx_scales[batch], "mix"
                )
                mix[unit] = acc

        def copy_mix_out(group):
            for unit in group:
                load, part = divmod(unit, LOAD_UNITS)
                tiles = slice(part * UNIT_TILES, (part + 1) * UNIT_TILES)
                nc.scalar.copy(out=rows_raws[load][:, tiles, 0:D], in_=mix[unit][:])

        def turn_comb(group):
            for unit in group:
                turned = turn(rows_raws[unit // LOAD_UNITS], unit, "comb_t")
                comb_t[unit] = turned

        def copy_comb_out(group):
            grouped = work.tile([P, len(group) * UNIT_ROWS, PACK], BF16, tag="comb", bufs=3, align_bytes=64)
            for unit in group:
                dst = grouped[:, rows_of(group, unit), :].bitcast(F32)
                src = comb_t[unit][:].rearrange("p u r -> p r u")
                if unit % 5 == 0:
                    nc.scalar.copy(out=dst, in_=src)
                else:
                    nc.vector.tensor_copy(out=dst, in_=src)
            comb[group[0]] = grouped

        def quantise_comb(group):
            codes, scales = quantise(comb[group[0]], group, "comb")
            comb_codes[group[0]], comb_scales[group[0]] = codes, scales

        def multiply_out(group):
            for unit in group:
                first_row = rows_of(group, unit).start
                acc = multiply(comb_codes[group[0]], comb_scales[group[0]], first_row, w_codes, w_scales, "out_acc")
                out_acc[unit] = acc

        def add_bias(group):
            summed = work.tile([P, len(group) * UNIT_TILES, D], F32, tag="result", bufs=7)
            width = 1 if group == GROUPS[-1] else UNIT_TILES
            for unit in group:
                for i in range(0, UNIT_TILES, width):
                    first = (unit - group[0]) * UNIT_TILES + i
                    nc.vector.tensor_tensor(
                        out=summed[:, first : first + width, :],
                        in0=out_acc[unit][:, i : i + width, :],
                        in1=bias[:].unsqueeze(1).to_broadcast([P, width, D]),
                        op=ADD,
                    )
            result[group[0]] = summed

        def tanh_and_store(group):
            batch, part = divmod(group[0], UNITS_PER_BATCH)
            out_rows = out[batch].rearrange("(p t) o -> p t o", t=BATCH_TILES)
            summed = result[group[0]]
            tiles = len(group) * UNIT_TILES
            width = 1 if group == GROUPS[-1] else tiles
            for i in range(0, tiles, width):
                piece = summed[:, i : i + width, :]
                nc.scalar.activation(out=piece, in_=piece, func=TANH)
                first = part * UNIT_TILES + i
                nc.sync.dma_start(out=out_rows[:, first : first + width, :], in_=piece)

        def run(stage, step):
            if 0 <= step < len(GROUPS):
                stage(GROUPS[step])

        def run_for_batch(stage, step):
            if 0 <= step < len(GROUPS):
                for unit in GROUPS[step]:
                    if unit % UNITS_PER_BATCH == 0:
                        stage(unit // UNITS_PER_BATCH)

        for step in range(len(GROUPS) + LAG_TANH):
            if step == W_STEP:
                prepare_w()
            run(turn_group_a, step)
            if step < WARM_STEPS:
                dummy_matmuls(1)
            run(multiply_mix, step - LAG_MIX)
            run(turn_comb, step - LAG_TURN_COMB)
            run(multiply_out, step - LAG_OUT)
            run(copy_a_out, step)
            run(copy_mix_out, step - LAG_MIX)
            run(add_bias, step - LAG_BIAS)
            run(tanh_and_store, step - LAG_TANH)
            run_for_batch(regroup_context, step if step == 0 else step + 2)
            run(quantise_comb, step - LAG_QUANTISE_COMB)
            run_for_batch(quantise_context, step)
            run(quantise_a, step)
            run(copy_comb_out, step - LAG_TURN_COMB)
